import numpy as np
import ml_dtypes


def mxq(x, axis, fmt="e4m3"):
    dtype, down = {"e4m3": (ml_dtypes.float8_e4m3fn, 7), "e5m2": (ml_dtypes.float8_e5m2, 14)}[fmt]
    v = np.moveaxis(np.asarray(x, np.float32).astype(ml_dtypes.bfloat16).astype(np.float64), axis, -1)
    blocks = v.reshape(v.shape[:-1] + (-1, 32))
    amax = np.abs(blocks).max(-1, keepdims=True)
    byte = np.maximum(np.where(amax > 0, np.frexp(amax)[1] - 1 + 127, 0) - down, 1)
    scale = np.exp2(byte - 127.0)
    codes = (blocks / scale).astype(np.float32).astype(dtype).astype(np.float64)
    return np.moveaxis((codes * scale).reshape(v.shape), -1, axis)


WIDE = False


def mx_kscale(k):
    if not WIDE:
        return np.ones(k)
    levels = np.array([10, -10, 5, -5, 0])
    if k % 512:
        return np.exp2(np.random.permutation(np.resize(levels, k // 32))).repeat(32)
    a = np.empty((k // 512, 16))
    for p in range(k // 512):
        a[p, :8] = np.random.permutation(np.resize(levels, 8))
        for g in range(8):
            far = levels[np.abs(levels - a[p, g]) >= 10]
            a[p, g + 8] = far[np.random.randint(len(far))]
    return np.exp2(a.ravel()).repeat(32)


BF16 = ml_dtypes.bfloat16


def bf(x):
    return np.asarray(x, np.float32).astype(BF16)


def f64(x):
    return np.asarray(x).astype(np.float64)


B, N, D, H, NS, SK1, SK2 = 1, 8192, 2048, 16, 10, 512, 1024


def sigmoid(v):
    return 1.0 / (1.0 + np.exp(-v))


def setup_inputs():
    s, t = mx_kscale(D), mx_kscale(D)
    return {"q_flat": bf(np.random.standard_normal((B, N, D)) * s),
            "gathered": bf(np.random.standard_normal((B, N, D)) * t),
            "Wgate": bf(np.random.standard_normal((D, D)) * D ** -0.5 / s[:, None]),
            "bgate": bf(2.0 + np.random.standard_normal(D) * 0.5),
            "Wout": bf(np.random.standard_normal((D, D)) * D ** -0.5 / t[:, None]),
            "bout": bf(np.random.standard_normal(D) * 0.2)}


def reference(q_flat, gathered, Wgate, bgate, Wout, bout):
    gate = sigmoid((mxq(f64(q_flat), 2, "e4m3") @ mxq(f64(Wgate), 0, "e4m3")) + f64(bgate))
    h = f64(gathered) * gate
    return (mxq(h, 2, "e4m3") @ mxq(f64(Wout), 0, "e4m3")) + f64(bout)

@@ -1,0 +1,247 @@
+from contextlib import ExitStack
+
+import concourse.mybir as mybir
+from concourse.masks import make_identity
+
+FLOPS = 2 * 2 * 8192 * 2048 * 2048
+
+F32 = mybir.dt.float32
+BF16 = mybir.dt.bfloat16
+U32 = mybir.dt.uint32
+U8 = mybir.dt.uint8
+FP8X4 = mybir.dt.float8_e4m3fn_x4
+SIGMOID = mybir.ActivationFunctionType.Sigmoid
+MULT = mybir.AluOpType.mult
+ADD = mybir.AluOpType.add
+
+P = 128
+STEPS = 64
+LAG = 4
+AHEAD = 2
+RAW_BUFS = 8
+GRP_BUFS = 6
+QC_BUFS = 8
+HC_BUFS = 9
+OUT_BUFS = 3
+
+
+def tile_causalwaveletfieldattentionh_pb_l_kernel(tc, q_flat, gathered, Wgate, bgate, Wout, bout, out):
+    nc = tc.nc
+    unit = "(b t p) (g c) -> b g p t c"
+    q_units = q_flat.flatten_outer_dims().rearrange(unit, t=4, p=P, c=512)
+    g_units = gathered.flatten_outer_dims().rearrange(unit, t=4, p=P, c=512)
+    out_units = out.flatten_outer_dims().rearrange(unit, t=4, p=P, c=512)
+    w_units = [
+        Wgate.rearrange("(k p j) (g c) -> g k p j c", p=P, j=4, c=512),
+        Wout.rearrange("(k p j) (g c) -> g k p j c", p=P, j=4, c=512),
+    ]
+
+    with ExitStack() as ctx:
+        const = ctx.enter_context(tc.tile_pool(name="const", bufs=1))
+        work = ctx.enter_context(tc.tile_pool(name="work", bufs=2))
+        acc_pool = ctx.enter_context(tc.psum_pool(name="accp", bufs=4))
+        tq_pool = ctx.enter_context(tc.psum_pool(name="tqp", bufs=2))
+        tg_pool = ctx.enter_context(tc.psum_pool(name="tgp", bufs=2))
+        ctx.enter_context(tc.manual_schedule())
+
+        raws = {}
+        grps = {}
+        wcodes = {}
+        qcodes = {}
+        hcodes = {}
+
+        def raw_tile():
+            return work.tile([P, 4, 512], BF16, name="raw", tag="raw", bufs=RAW_BUFS, align_bytes=64)
+
+        def grp_tile():
+            return work.tile([P, 512, 4], BF16, name="grp", tag="grp", bufs=GRP_BUFS, align_bytes=64)
+
+        def load(key, src):
+            t = raw_tile()
+            nc.sync.dma_start(out=t[:], in_=src)
+            raws[key] = t
+
+        def load_w(w, k):
+            if w < 8:
+                load(("w", w, k), w_units[w // 4][w % 4, k])
+
+        def issue_loads(step):
+            if step == -1:
+                for k in range(4):
+                    load(("q", k), q_units[0, k])
+                    load_w(0, k)
+            else:
+                load_w(step + 1, 0)
+                load_w(step + 1, 1)
+                if step < STEPS:
+                    load(("g", step), g_units[step // 4, step % 4])
+                if step + 4 < STEPS:
+                    load(("q", step + 4), q_units[(step + 4) // 4, step % 4])
+            load_w(step + 2, 2)
+            load_w(step + 2, 3)
+
+        def transposes(key, pool, tag):
+            words = raws[key][:].rearrange("p t c -> p (t c)").bitcast(F32)
+            banks = []
+            for j in range(2):
+                xt = pool.tile([P, 2, 256], F32, name=tag, tag=tag)
+                for u in range(2):
+                    for i in range(2):
+                        tt = 2 * j + i
+                        nc.tensor.transpose(
+                            xt[:, u, i * P : (i + 1) * P],
+                            words[:, tt * 256 + u : (tt + 1) * 256 : 2],
+                            ident[:],
+                        )
+                banks.append(xt)
+            return banks
+
+        def quantize(grp, tag, bufs):
+            pool = const if bufs == 1 else work
+            codes = pool.tile([P, 512], U32, name=tag + "c", tag=tag + "c", bufs=bufs, align_bytes=64)
+            scales = pool.tile([P, 512], U8, name=tag + "s", tag=tag + "s", bufs=bufs, align_bytes=64)
+            nc.vector.quantize_mx(
+                out=codes[:].bitcast(FP8X4), scales=scales[:], in_=grp[:].rearrange("p r j -> p (r j)")
+            )
+            return codes, scales
+
+        def w_copy(w, k, copy):
+            if w >= 8:
+                return
+            raw = raws[("w", w, k)]
+            grp = grp_tile()
+            if w < 4:
+                copy(
+                    out=grp[:].rearrange("p (t m) j -> p t m j", t=4),
+                    in_=raw[:].rearrange("p j (m t) -> p t m j", t=4),
+                )
+            else:
+                copy(out=grp[:], in_=raw[:].rearrange("p j c -> p c j"))
+            grps[(w, k)] = grp
+
+        def w_quant(w, k):
+            if w < 8:
+                wcodes[(w, k)] = quantize(grps[(w, k)], "w%d%d" % (w, k), 1)
+
+        def q_transposes(u):
+            banks = transposes(("q", u), tq_pool, "tq")
+            grp = grp_tile()
+            words = grp[:].rearrange("p r j -> p (r j)").bitcast(F32).rearrange("p (r u) -> p r u", u=2)
+            for j in range(2):
+                nc.scalar.copy(out=words[:, j * 256 : (j + 1) * 256, :], in_=banks[j][:].rearrange("p u r -> p r u"))
+            return grp
+
+        def mx_group(lhs, rhs, lcols, rcols):
+            acc = acc_pool.tile([P, 512], F32, name="acc", tag="acc")
+            for k in range(4):
+                nc.tensor.matmul_mx(
+                    out=acc[:],
+                    lhsT=lhs[k][0][:, lcols].bitcast(FP8X4),
+                    lhsT_scale=lhs[k][1][:, lcols],
+                    rhs=rhs[k][0][:, rcols].bitcast(FP8X4),
+                    rhs_scale=rhs[k][1][:, rcols],
+                    start=(k == 0),
+                    stop=(k == 3),
+                )
+            return acc
+
+        bg_bf = const.tile([P, 4, 4], BF16, name="bg_bf", tag="bg_bf")
+        nc.scalar.dma_start(out=bg_bf[:], in_=bgate.rearrange("(g p t) -> p g t", p=P, t=4))
+        bo_src = raw_tile()
+        nc.gpsimd.memset(bo_src[:], 0.0)
+        nc.scalar.dma_start(
+            out=bo_src[0:1].rearrange("p t c -> p (t c)"), in_=bout.rearrange("(o c) -> o c", o=1)
+        )
+        warm_in = const.tile([P, 1], F32, name="warm_in", tag="warm_in")
+        warm_out = const.tile([P, 1], F32, name="warm_out", tag="warm_out")
+        nc.vector.memset(warm_in[:], 0.0)
+        nc.scalar.activation(out=warm_out[:], in_=warm_in[:], func=SIGMOID)
+        ident = const.tile([P, P], F32, name="ident", tag="ident")
+        make_identity(nc, ident[:])
+        ones = const.tile([P, P], BF16, name="ones", tag="ones")
+        nc.gpsimd.memset(ones[:], 1.0)
+        bg = const.tile([P, 16], F32, name="bg", tag="bg")
+        nc.vector.tensor_copy(out=bg[:], in_=bg_bf[:].rearrange("p g t -> p (g t)"))
+        bo = const.tile([P, 4, 512], F32, name="bo", tag="bo")
+
+        for step in range(-1, AHEAD):
+            issue_loads(step)
+
+        for k in range(4):
+            qg = q_transposes(k)
+            if k == 0:
+                for n in range(4):
+                    acc = acc_pool.tile([P, 512], F32, name="acc", tag="acc")
+                    nc.tensor.matmul(out=acc[:], lhsT=ones[:], rhs=bo_src[:, n, :], start=True, stop=True)
+                    nc.vector.tensor_copy(out=bo[:, n, :], in_=acc[:])
+            w_copy(0, k, nc.vector.tensor_copy)
+            if k > 0:
+                w_quant(0, k - 1)
+            qcodes[k] = quantize(qg, "q", QC_BUFS)
+        w_quant(0, 3)
+        w_copy(1, 2, nc.scalar.copy)
+        w_copy(1, 3, nc.scalar.copy)
+
+        for s in range(STEPS + LAG):
+            issue_loads(s + AHEAD)
+
+            w_copy(s + 1, 0, nc.vector.tensor_copy)
+            w_copy(s + 1, 1, nc.vector.tensor_copy)
+            for k in (2, 0, 3, 1):
+                w_quant(s + 1, k)
+
+            if s < STEPS:
+                b, g = divmod(s, 4)
+                sig = work.tile([P, 4, 512], F32, name="sig", tag="sig", bufs=2)
+                for t in range(4):
+                    acc = mx_group(
+                        [wcodes[(g, k)] for k in range(4)],
+                        [qcodes[4 * b + k] for k in range(4)],
+                        slice(t * P, (t + 1) * P),
+                        slice(0, 512),
+                    )
+                    nc.scalar.activation(
+                        out=sig[:, t, :], in_=acc[:], func=SIGMOID, bias=bg[:, 4 * g + t : 4 * g + t + 1]
+                    )
+                g_banks = transposes(("g", s), tg_pool, "tg")
+            if s + 4 < STEPS:
+                qg = q_transposes(s + 4)
+            w_copy(s + 2, 2, nc.scalar.copy)
+            w_copy(s + 2, 3, nc.scalar.copy)
+
+            if s < STEPS:
+                hg = grp_tile()
+                for j in range(2):
+                    rows = slice(j * 256, (j + 1) * 256)
+                    nc.vector.tensor_tensor(
+                        out=hg[:, rows, :].rearrange("p r (u e) -> p r u e", e=2),
+                        in0=sig[:, :, rows].rearrange("p (u e) r -> p r u e", e=2),
+                        in1=g_banks[j][:]
+                        .rearrange("p u r -> p (u r)")
+                        .bitcast(BF16)
+                        .rearrange("p (u r e) -> p r u e", u=2, e=2),
+                        op=MULT,
+                    )
+            if s + 4 < STEPS:
+                qcodes[s + 4] = quantize(qg, "q", QC_BUFS)
+
+            if s >= LAG:
+                b2, n = divmod(s - LAG, 4)
+                last = s == STEPS + LAG - 1
+                ost = work.tile([P, 4, 512], F32, name="ost", tag="ost", bufs=OUT_BUFS)
+                for tt in range(4):
+                    acc = mx_group(
+                        [hcodes[4 * b2 + k] for k in range(4)],
+                        [wcodes[(4 + n, k)] for k in range(4)],
+                        slice(tt * P, (tt + 1) * P),
+                        slice(0, 512),
+                    )
+                    nc.vector.tensor_tensor(out=ost[:, tt, :], in0=acc[:], in1=bo[:, n, :], op=ADD)
+                    if tt == 0 and s < STEPS:
+                        hcodes[s] = quantize(hg, "h", HC_BUFS)
+                    if last:
+                        nc.sync.dma_start(out=out_units[b2, n][:, tt, :], in_=ost[:, tt, :])
+                if not last:
+                    nc.sync.dma_start(out=out_units[b2, n], in_=ost[:])
+            else:
+                hcodes[s] = quantize(hg, "h", HC_BUFS)

@@ -18,11 +18,13 @@ P = 128
 STEPS = 64
 LAG = 4
 AHEAD = 2
+SORT_FROM = 7
 RAW_BUFS = 8
-GRP_BUFS = 6
+SRT_BUFS = 4
+GRP_BUFS = 5
 QC_BUFS = 8
 HC_BUFS = 9
-OUT_BUFS = 3
+OUT_BUFS = 2
 
 
 def tile_causalwaveletfieldattentionh_pb_l_kernel(tc, q_flat, gathered, Wgate, bgate, Wout, bout, out):
@@ -45,6 +47,7 @@ def tile_causalwaveletfieldattentionh_pb_l_kernel(tc, q_flat, gathered, Wgate, b
         ctx.enter_context(tc.manual_schedule())
 
         raws = {}
+        srts = {}
         grps = {}
         wcodes = {}
         qcodes = {}
@@ -65,6 +68,12 @@ def tile_causalwaveletfieldattentionh_pb_l_kernel(tc, q_flat, gathered, Wgate, b
             if w < 8:
                 load(("w", w, k), w_units[w // 4][w % 4, k])
 
+        def load_units(step):
+            if step + 4 < STEPS:
+                load(("q", step + 4), q_units[(step + 4) // 4, step % 4])
+            if step < STEPS:
+                load(("g", step), g_units[step // 4, step % 4])
+
         def issue_loads(step):
             if step == -1:
                 for k in range(4):
@@ -73,12 +82,18 @@ def tile_causalwaveletfieldattentionh_pb_l_kernel(tc, q_flat, gathered, Wgate, b
             else:
                 load_w(step + 1, 0)
                 load_w(step + 1, 1)
-                if step < STEPS:
-                    load(("g", step), g_units[step // 4, step % 4])
-                if step + 4 < STEPS:
-                    load(("q", step + 4), q_units[(step + 4) // 4, step % 4])
+                if step < SORT_FROM:
+                    load_units(step)
+            if step + 1 >= SORT_FROM:
+                load_units(step + 1)
             load_w(step + 2, 2)
             load_w(step + 2, 3)
+
+        def sort_words(key):
+            words = raws[key][:].rearrange("p t c -> p (t c)").bitcast(F32)
+            srt = work.tile([P, 4, 2, P], F32, name="srt", tag="srt", bufs=SRT_BUFS)
+            nc.scalar.copy(out=srt[:], in_=words.rearrange("p (t m u) -> p t u m", t=4, u=2))
+            srts[key] = srt
 
         def transposes(key, pool, tag):
             words = raws[key][:].rearrange("p t c -> p (t c)").bitcast(F32)
@@ -88,11 +103,11 @@ def tile_causalwaveletfieldattentionh_pb_l_kernel(tc, q_flat, gathered, Wgate, b
                 for u in range(2):
                     for i in range(2):
                         tt = 2 * j + i
-                        nc.tensor.transpose(
-                            xt[:, u, i * P : (i + 1) * P],
-                            words[:, tt * 256 + u : (tt + 1) * 256 : 2],
-                            ident[:],
-                        )
+                        if key in srts:
+                            src = srts[key][:, tt, u, :]
+                        else:
+                            src = words[:, tt * 256 + u : (tt + 1) * 256 : 2]
+                        nc.tensor.transpose(xt[:, u, i * P : (i + 1) * P], src, ident[:])
                 banks.append(xt)
             return banks
 
@@ -131,19 +146,23 @@ def tile_causalwaveletfieldattentionh_pb_l_kernel(tc, q_flat, gathered, Wgate, b
                 nc.scalar.copy(out=words[:, j * 256 : (j + 1) * 256, :], in_=banks[j][:].rearrange("p u r -> p r u"))
             return grp
 
-        def mx_group(lhs, rhs, lcols, rcols):
-            acc = acc_pool.tile([P, 512], F32, name="acc", tag="acc")
-            for k in range(4):
+        def mx_groups(lhs, rhs, k_outer):
+            accs = [acc_pool.tile([P, 512], F32, name="acc", tag="acc") for i in range(4)]
+            if k_outer:
+                passes = [(i, k) for k in range(4) for i in range(4)]
+            else:
+                passes = [(i, k) for i in range(4) for k in range(4)]
+            for i, k in passes:
                 nc.tensor.matmul_mx(
-                    out=acc[:],
-                    lhsT=lhs[k][0][:, lcols].bitcast(FP8X4),
-                    lhsT_scale=lhs[k][1][:, lcols],
-                    rhs=rhs[k][0][:, rcols].bitcast(FP8X4),
-                    rhs_scale=rhs[k][1][:, rcols],
+                    out=accs[i][:],
+                    lhsT=lhs[k][0][:, i * P : (i + 1) * P].bitcast(FP8X4),
+                    lhsT_scale=lhs[k][1][:, i * P : (i + 1) * P],
+                    rhs=rhs[k][0][:].bitcast(FP8X4),
+                    rhs_scale=rhs[k][1][:],
                     start=(k == 0),
                     stop=(k == 3),
                 )
-            return acc
+            return accs
 
         bg_bf = const.tile([P, 4, 4], BF16, name="bg_bf", tag="bg_bf")
         nc.scalar.dma_start(out=bg_bf[:], in_=bgate.rearrange("(g p t) -> p g t", p=P, t=4))
@@ -175,10 +194,8 @@ def tile_causalwaveletfieldattentionh_pb_l_kernel(tc, q_flat, gathered, Wgate, b
                     nc.tensor.matmul(out=acc[:], lhsT=ones[:], rhs=bo_src[:, n, :], start=True, stop=True)
                     nc.vector.tensor_copy(out=bo[:, n, :], in_=acc[:])
             w_copy(0, k, nc.vector.tensor_copy)
-            if k > 0:
-                w_quant(0, k - 1)
             qcodes[k] = quantize(qg, "q", QC_BUFS)
-        w_quant(0, 3)
+            w_quant(0, k)
         w_copy(1, 2, nc.scalar.copy)
         w_copy(1, 3, nc.scalar.copy)
 
@@ -193,19 +210,23 @@ def tile_causalwaveletfieldattentionh_pb_l_kernel(tc, q_flat, gathered, Wgate, b
             if s < STEPS:
                 b, g = divmod(s, 4)
                 sig = work.tile([P, 4, 512], F32, name="sig", tag="sig", bufs=2)
+                accs = mx_groups(
+                    [wcodes[(g, k)] for k in range(4)], [qcodes[4 * b + k] for k in range(4)], s == 0
+                )
                 for t in range(4):
-                    acc = mx_group(
-                        [wcodes[(g, k)] for k in range(4)],
-                        [qcodes[4 * b + k] for k in range(4)],
-                        slice(t * P, (t + 1) * P),
-                        slice(0, 512),
-                    )
                     nc.scalar.activation(
-                        out=sig[:, t, :], in_=acc[:], func=SIGMOID, bias=bg[:, 4 * g + t : 4 * g + t + 1]
+                        out=sig[:, t, :], in_=accs[t][:], func=SIGMOID, bias=bg[:, 4 * g + t : 4 * g + t + 1]
                     )
-                g_banks = transposes(("g", s), tg_pool, "tg")
             if s + 4 < STEPS:
                 qg = q_transposes(s + 4)
+                qcodes[s + 4] = quantize(qg, "q", QC_BUFS)
+            if s < STEPS:
+                g_banks = transposes(("g", s), tg_pool, "tg")
+            if s + 1 >= SORT_FROM:
+                if s + 5 < STEPS:
+                    sort_words(("q", s + 5))
+                if s + 1 < STEPS:
+                    sort_words(("g", s + 1))
             w_copy(s + 2, 2, nc.scalar.copy)
             w_copy(s + 2, 3, nc.scalar.copy)
 
@@ -222,21 +243,16 @@ def tile_causalwaveletfieldattentionh_pb_l_kernel(tc, q_flat, gathered, Wgate, b
                         .rearrange("p (u r e) -> p r u e", u=2, e=2),
                         op=MULT,
                     )
-            if s + 4 < STEPS:
-                qcodes[s + 4] = quantize(qg, "q", QC_BUFS)
 
             if s >= LAG:
                 b2, n = divmod(s - LAG, 4)
                 last = s == STEPS + LAG - 1
                 ost = work.tile([P, 4, 512], F32, name="ost", tag="ost", bufs=OUT_BUFS)
+                accs = mx_groups(
+                    [hcodes[4 * b2 + k] for k in range(4)], [wcodes[(4 + n, k)] for k in range(4)], False
+                )
                 for tt in range(4):
-                    acc = mx_group(
-                        [hcodes[4 * b2 + k] for k in range(4)],
-                        [wcodes[(4 + n, k)] for k in range(4)],
-                        slice(tt * P, (tt + 1) * P),
-                        slice(0, 512),
-                    )
-                    nc.vector.tensor_tensor(out=ost[:, tt, :], in0=acc[:], in1=bo[:, n, :], op=ADD)
+                    nc.vector.tensor_tensor(out=ost[:, tt, :], in0=accs[tt][:], in1=bo[:, n, :], op=ADD)
                     if tt == 0 and s < STEPS:
                         hcodes[s] = quantize(hg, "h", HC_BUFS)
                     if last:

@@ -16,14 +16,14 @@ ADD = mybir.AluOpType.add
 
 P = 128
 STEPS = 64
-LAG = 4
+LAG = 5
 AHEAD = 2
-SORT_FROM = 7
+SORT_FROM = 8
 RAW_BUFS = 8
 SRT_BUFS = 4
 GRP_BUFS = 5
 QC_BUFS = 8
-HC_BUFS = 9
+HC_BUFS = 10
 OUT_BUFS = 2
 
 
@@ -41,9 +41,9 @@ def tile_causalwaveletfieldattentionh_pb_l_kernel(tc, q_flat, gathered, Wgate, b
     with ExitStack() as ctx:
         const = ctx.enter_context(tc.tile_pool(name="const", bufs=1))
         work = ctx.enter_context(tc.tile_pool(name="work", bufs=2))
-        acc_pool = ctx.enter_context(tc.psum_pool(name="accp", bufs=4))
+        acc_pool = ctx.enter_context(tc.psum_pool(name="accp", bufs=3))
         tq_pool = ctx.enter_context(tc.psum_pool(name="tqp", bufs=2))
-        tg_pool = ctx.enter_context(tc.psum_pool(name="tgp", bufs=2))
+        tg_pool = ctx.enter_context(tc.psum_pool(name="tgp", bufs=3))
         ctx.enter_context(tc.manual_schedule())
 
         raws = {}
@@ -64,6 +64,10 @@ def tile_causalwaveletfieldattentionh_pb_l_kernel(tc, q_flat, gathered, Wgate, b
             nc.sync.dma_start(out=t[:], in_=src)
             raws[key] = t
 
+        prep = {}
+        for w in range(8):
+            prep[(w if w < 4 else LAG + w - 4) - 1] = w
+
         def load_w(w, k):
             if w < 8:
                 load(("w", w, k), w_units[w // 4][w % 4, k])
@@ -80,14 +84,14 @@ def tile_causalwaveletfieldattentionh_pb_l_kernel(tc, q_flat, gathered, Wgate, b
                     load(("q", k), q_units[0, k])
                     load_w(0, k)
             else:
-                load_w(step + 1, 0)
-                load_w(step + 1, 1)
+                load_w(prep.get(step, 8), 0)
+                load_w(prep.get(step, 8), 1)
                 if step < SORT_FROM:
                     load_units(step)
             if step + 1 >= SORT_FROM:
                 load_units(step + 1)
-            load_w(step + 2, 2)
-            load_w(step + 2, 3)
+            load_w(prep.get(step + 1, 8), 2)
+            load_w(prep.get(step + 1, 8), 3)
 
         def sort_words(key):
             words = raws[key][:].rearrange("p t c -> p (t c)").bitcast(F32)
@@ -146,13 +150,9 @@ def tile_causalwaveletfieldattentionh_pb_l_kernel(tc, q_flat, gathered, Wgate, b
                 nc.scalar.copy(out=words[:, j * 256 : (j + 1) * 256, :], in_=banks[j][:].rearrange("p u r -> p r u"))
             return grp
 
-        def mx_groups(lhs, rhs, k_outer):
+        def mx_groups(lhs, rhs):
             accs = [acc_pool.tile([P, 512], F32, name="acc", tag="acc") for i in range(4)]
-            if k_outer:
-                passes = [(i, k) for k in range(4) for i in range(4)]
-            else:
-                passes = [(i, k) for i in range(4) for k in range(4)]
-            for i, k in passes:
+            for i, k in [(i, k) for i in range(4) for k in range(4)]:
                 nc.tensor.matmul_mx(
                     out=accs[i][:],
                     lhsT=lhs[k][0][:, i * P : (i + 1) * P].bitcast(FP8X4),
@@ -163,6 +163,21 @@ def tile_causalwaveletfieldattentionh_pb_l_kernel(tc, q_flat, gathered, Wgate, b
                     stop=(k == 3),
                 )
             return accs
+
+        def multiply(sig, g_banks):
+            hg = grp_tile()
+            for j in range(2):
+                rows = slice(j * 256, (j + 1) * 256)
+                nc.vector.tensor_tensor(
+                    out=hg[:, rows, :].rearrange("p r (u e) -> p r u e", e=2),
+                    in0=sig[:, :, rows].rearrange("p (u e) r -> p r u e", e=2),
+                    in1=g_banks[j][:]
+                    .rearrange("p u r -> p (u r)")
+                    .bitcast(BF16)
+                    .rearrange("p (u r e) -> p r u e", u=2, e=2),
+                    op=MULT,
+                )
+            return hg
 
         bg_bf = const.tile([P, 4, 4], BF16, name="bg_bf", tag="bg_bf")
         nc.scalar.dma_start(out=bg_bf[:], in_=bgate.rearrange("(g p t) -> p g t", p=P, t=4))
@@ -202,16 +217,18 @@ def tile_causalwaveletfieldattentionh_pb_l_kernel(tc, q_flat, gathered, Wgate, b
         for s in range(STEPS + LAG):
             issue_loads(s + AHEAD)
 
-            w_copy(s + 1, 0, nc.vector.tensor_copy)
-            w_copy(s + 1, 1, nc.vector.tensor_copy)
+            w_copy(prep.get(s, 8), 0, nc.vector.tensor_copy)
+            w_copy(prep.get(s, 8), 1, nc.vector.tensor_copy)
             for k in (2, 0, 3, 1):
-                w_quant(s + 1, k)
+                w_quant(prep.get(s, 8), k)
 
+            if 1 <= s <= STEPS:
+                hg = multiply(sig, g_banks)
             if s < STEPS:
                 b, g = divmod(s, 4)
                 sig = work.tile([P, 4, 512], F32, name="sig", tag="sig", bufs=2)
                 accs = mx_groups(
-                    [wcodes[(g, k)] for k in range(4)], [qcodes[4 * b + k] for k in range(4)], s == 0
+                    [wcodes[(g, k)] for k in range(4)], [qcodes[4 * b + k] for k in range(4)]
                 )
                 for t in range(4):
                     nc.scalar.activation(
@@ -220,6 +237,8 @@ def tile_causalwaveletfieldattentionh_pb_l_kernel(tc, q_flat, gathered, Wgate, b
             if s + 4 < STEPS:
                 qg = q_transposes(s + 4)
                 qcodes[s + 4] = quantize(qg, "q", QC_BUFS)
+            if 1 <= s <= STEPS:
+                hcodes[s - 1] = quantize(hg, "h", HC_BUFS)
             if s < STEPS:
                 g_banks = transposes(("g", s), tg_pool, "tg")
             if s + 1 >= SORT_FROM:
@@ -227,37 +246,19 @@ def tile_causalwaveletfieldattentionh_pb_l_kernel(tc, q_flat, gathered, Wgate, b
                     sort_words(("q", s + 5))
                 if s + 1 < STEPS:
                     sort_words(("g", s + 1))
-            w_copy(s + 2, 2, nc.scalar.copy)
-            w_copy(s + 2, 3, nc.scalar.copy)
-
-            if s < STEPS:
-                hg = grp_tile()
-                for j in range(2):
-                    rows = slice(j * 256, (j + 1) * 256)
-                    nc.vector.tensor_tensor(
-                        out=hg[:, rows, :].rearrange("p r (u e) -> p r u e", e=2),
-                        in0=sig[:, :, rows].rearrange("p (u e) r -> p r u e", e=2),
-                        in1=g_banks[j][:]
-                        .rearrange("p u r -> p (u r)")
-                        .bitcast(BF16)
-                        .rearrange("p (u r e) -> p r u e", u=2, e=2),
-                        op=MULT,
-                    )
+            w_copy(prep.get(s + 1, 8), 2, nc.scalar.copy)
+            w_copy(prep.get(s + 1, 8), 3, nc.scalar.copy)
 
             if s >= LAG:
                 b2, n = divmod(s - LAG, 4)
                 last = s == STEPS + LAG - 1
                 ost = work.tile([P, 4, 512], F32, name="ost", tag="ost", bufs=OUT_BUFS)
                 accs = mx_groups(
-                    [hcodes[4 * b2 + k] for k in range(4)], [wcodes[(4 + n, k)] for k in range(4)], False
+                    [hcodes[4 * b2 + k] for k in range(4)], [wcodes[(4 + n, k)] for k in range(4)]
                 )
                 for tt in range(4):
                     nc.vector.tensor_tensor(out=ost[:, tt, :], in0=accs[tt][:], in1=bo[:, n, :], op=ADD)
-                    if tt == 0 and s < STEPS:
-                        hcodes[s] = quantize(hg, "h", HC_BUFS)
                     if last:
                         nc.sync.dma_start(out=out_units[b2, n][:, tt, :], in_=ost[:, tt, :])
                 if not last:
                     nc.sync.dma_start(out=out_units[b2, n], in_=ost[:])
-            else:
-                hcodes[s] = quantize(hg, "h", HC_BUFS)

@@ -15,25 +15,43 @@ MULT = mybir.AluOpType.mult
 ADD = mybir.AluOpType.add
 
 P = 128
+ORDER = [(s % 2, s // 2) for s in range(8)] + [(b, g) for b in range(2, 16) for g in range(4)]
 STEPS = 64
-LAG = 5
+LAG = 8
 AHEAD = 2
 SORT_FROM = 8
 RAW_BUFS = 8
 SRT_BUFS = 4
 GRP_BUFS = 5
-QC_BUFS = 8
-HC_BUFS = 10
+QC_BUFS = 11
+QS_BUFS = 4
+HC_BUFS = 14
+HS_BUFS = 5
 OUT_BUFS = 2
+
+
+def q_units(step):
+    if step <= 0:
+        return [4 * (step + 1) + k for k in range(4)]
+    if 3 <= step < STEPS - 5:
+        return [step + 5]
+    return []
+
+
+def w_unit(step, half):
+    x = 4 + 2 * step + half
+    if step < 0 or x >= 32:
+        return None
+    return divmod(x, 4)
 
 
 def tile_causalwaveletfieldattentionh_pb_l_kernel(tc, q_flat, gathered, Wgate, bgate, Wout, bout, out):
     nc = tc.nc
     unit = "(b t p) (g c) -> b g p t c"
-    q_units = q_flat.flatten_outer_dims().rearrange(unit, t=4, p=P, c=512)
-    g_units = gathered.flatten_outer_dims().rearrange(unit, t=4, p=P, c=512)
-    out_units = out.flatten_outer_dims().rearrange(unit, t=4, p=P, c=512)
-    w_units = [
+    q_view = q_flat.flatten_outer_dims().rearrange(unit, t=4, p=P, c=512)
+    g_view = gathered.flatten_outer_dims().rearrange(unit, t=4, p=P, c=512)
+    out_view = out.flatten_outer_dims().rearrange(unit, t=4, p=P, c=512)
+    w_view = [
         Wgate.rearrange("(k p j) (g c) -> g k p j c", p=P, j=4, c=512),
         Wout.rearrange("(k p j) (g c) -> g k p j c", p=P, j=4, c=512),
     ]
@@ -41,17 +59,16 @@ def tile_causalwaveletfieldattentionh_pb_l_kernel(tc, q_flat, gathered, Wgate, b
     with ExitStack() as ctx:
         const = ctx.enter_context(tc.tile_pool(name="const", bufs=1))
         work = ctx.enter_context(tc.tile_pool(name="work", bufs=2))
-        acc_pool = ctx.enter_context(tc.psum_pool(name="accp", bufs=3))
+        acc_pool = ctx.enter_context(tc.psum_pool(name="accp", bufs=4))
         tq_pool = ctx.enter_context(tc.psum_pool(name="tqp", bufs=2))
-        tg_pool = ctx.enter_context(tc.psum_pool(name="tgp", bufs=3))
+        tg_pool = ctx.enter_context(tc.psum_pool(name="tgp", bufs=2))
         ctx.enter_context(tc.manual_schedule())
 
         raws = {}
         srts = {}
         grps = {}
-        wcodes = {}
-        qcodes = {}
-        hcodes = {}
+        codes = {}
+        planes = {}
 
         def raw_tile():
             return work.tile([P, 4, 512], BF16, name="raw", tag="raw", bufs=RAW_BUFS, align_bytes=64)
@@ -64,34 +81,25 @@ def tile_causalwaveletfieldattentionh_pb_l_kernel(tc, q_flat, gathered, Wgate, b
             nc.sync.dma_start(out=t[:], in_=src)
             raws[key] = t
 
-        prep = {}
-        for w in range(8):
-            prep[(w if w < 4 else LAG + w - 4) - 1] = w
+        def load_w(wk):
+            if wk is not None:
+                load(("w", wk), w_view[wk[0] // 4][wk[0] % 4, wk[1]])
 
-        def load_w(w, k):
-            if w < 8:
-                load(("w", w, k), w_units[w // 4][w % 4, k])
-
-        def load_units(step):
-            if step + 4 < STEPS:
-                load(("q", step + 4), q_units[(step + 4) // 4, step % 4])
+        def load_step(step):
+            for u in q_units(step):
+                load(("q", u), q_view[u // 4, u % 4])
             if step < STEPS:
-                load(("g", step), g_units[step // 4, step % 4])
+                load(("g", step), g_view[ORDER[step][0], ORDER[step][1]])
 
         def issue_loads(step):
             if step == -1:
                 for k in range(4):
-                    load(("q", k), q_units[0, k])
-                    load_w(0, k)
+                    load(("q", k), q_view[0, k])
+                    load_w((0, k))
             else:
-                load_w(prep.get(step, 8), 0)
-                load_w(prep.get(step, 8), 1)
-                if step < SORT_FROM:
-                    load_units(step)
-            if step + 1 >= SORT_FROM:
-                load_units(step + 1)
-            load_w(prep.get(step + 1, 8), 2)
-            load_w(prep.get(step + 1, 8), 3)
+                load_w(w_unit(step, 0))
+                load_step(step)
+            load_w(w_unit(step + 1, 1))
 
         def sort_words(key):
             words = raws[key][:].rearrange("p t c -> p (t c)").bitcast(F32)
@@ -115,32 +123,40 @@ def tile_causalwaveletfieldattentionh_pb_l_kernel(tc, q_flat, gathered, Wgate, b
                 banks.append(xt)
             return banks
 
-        def quantize(grp, tag, bufs):
-            pool = const if bufs == 1 else work
-            codes = pool.tile([P, 512], U32, name=tag + "c", tag=tag + "c", bufs=bufs, align_bytes=64)
-            scales = pool.tile([P, 512], U8, name=tag + "s", tag=tag + "s", bufs=bufs, align_bytes=64)
+        def quantize(grp, kind, group, k):
+            if kind == "w":
+                pool, tag, cbufs, sbufs = const, "w%d" % group, 1, 1
+                ctag = "w%d%d" % (group, k)
+            else:
+                pool, tag, ctag = work, kind + "s", kind + "c"
+                cbufs, sbufs = (QC_BUFS, QS_BUFS) if kind == "q" else (HC_BUFS, HS_BUFS)
+            if (kind, group) not in planes:
+                planes[(kind, group)] = pool.tile([P, 512], U8, name=tag, tag=tag, bufs=sbufs, align_bytes=64)
+            c = pool.tile([P, 512], U32, name=ctag, tag=ctag, bufs=cbufs, align_bytes=64)
             nc.vector.quantize_mx(
-                out=codes[:].bitcast(FP8X4), scales=scales[:], in_=grp[:].rearrange("p r j -> p (r j)")
+                out=c[:].bitcast(FP8X4),
+                scales=planes[(kind, group)][4 * k : P, :],
+                in_=grp[:].rearrange("p r j -> p (r j)"),
             )
-            return codes, scales
+            codes[(kind, group, k)] = c
 
-        def w_copy(w, k, copy):
-            if w >= 8:
+        def w_copy(wk, copy):
+            if wk is None:
                 return
-            raw = raws[("w", w, k)]
+            raw = raws[("w", wk)]
             grp = grp_tile()
-            if w < 4:
+            if wk[0] < 4:
                 copy(
                     out=grp[:].rearrange("p (t m) j -> p t m j", t=4),
                     in_=raw[:].rearrange("p j (m t) -> p t m j", t=4),
                 )
             else:
                 copy(out=grp[:], in_=raw[:].rearrange("p j c -> p c j"))
-            grps[(w, k)] = grp
+            grps[wk] = grp
 
-        def w_quant(w, k):
-            if w < 8:
-                wcodes[(w, k)] = quantize(grps[(w, k)], "w%d%d" % (w, k), 1)
+        def w_quant(wk):
+            if wk is not None:
+                quantize(grps[wk], "w", wk[0], wk[1])
 
         def q_transposes(u):
             banks = transposes(("q", u), tq_pool, "tq")
@@ -150,34 +166,31 @@ def tile_causalwaveletfieldattentionh_pb_l_kernel(tc, q_flat, gathered, Wgate, b
                 nc.scalar.copy(out=words[:, j * 256 : (j + 1) * 256, :], in_=banks[j][:].rearrange("p u r -> p r u"))
             return grp
 
-        def mx_groups(lhs, rhs):
-            accs = [acc_pool.tile([P, 512], F32, name="acc", tag="acc") for i in range(4)]
-            for i, k in [(i, k) for i in range(4) for k in range(4)]:
+        def mx_group(lhs, rhs, i):
+            acc = acc_pool.tile([P, 512], F32, name="acc", tag="acc")
+            for k in range(4):
                 nc.tensor.matmul_mx(
-                    out=accs[i][:],
-                    lhsT=lhs[k][0][:, i * P : (i + 1) * P].bitcast(FP8X4),
-                    lhsT_scale=lhs[k][1][:, i * P : (i + 1) * P],
-                    rhs=rhs[k][0][:].bitcast(FP8X4),
-                    rhs_scale=rhs[k][1][:],
+                    out=acc[:],
+                    lhsT=codes[lhs + (k,)][:, i * P : (i + 1) * P].bitcast(FP8X4),
+                    lhsT_scale=planes[lhs][4 * k : P, i * P : (i + 1) * P],
+                    rhs=codes[rhs + (k,)][:].bitcast(FP8X4),
+                    rhs_scale=planes[rhs][4 * k : P, :],
                     start=(k == 0),
                     stop=(k == 3),
                 )
-            return accs
+            return acc
 
-        def multiply(sig, g_banks):
-            hg = grp_tile()
-            for j in range(2):
-                rows = slice(j * 256, (j + 1) * 256)
-                nc.vector.tensor_tensor(
-                    out=hg[:, rows, :].rearrange("p r (u e) -> p r u e", e=2),
-                    in0=sig[:, :, rows].rearrange("p (u e) r -> p r u e", e=2),
-                    in1=g_banks[j][:]
-                    .rearrange("p u r -> p (u r)")
-                    .bitcast(BF16)
-                    .rearrange("p (u r e) -> p r u e", u=2, e=2),
-                    op=MULT,
-                )
-            return hg
+        def multiply(hg, sig, g_banks, j):
+            rows = slice(j * 256, (j + 1) * 256)
+            nc.vector.tensor_tensor(
+                out=hg[:, rows, :].rearrange("p r (u e) -> p r u e", e=2),
+                in0=sig[:, :, rows].rearrange("p (u e) r -> p r u e", e=2),
+                in1=g_banks[j][:]
+                .rearrange("p u r -> p (u r)")
+                .bitcast(BF16)
+                .rearrange("p (u r e) -> p r u e", u=2, e=2),
+                op=MULT,
+            )
 
         bg_bf = const.tile([P, 4, 4], BF16, name="bg_bf", tag="bg_bf")
         nc.scalar.dma_start(out=bg_bf[:], in_=bgate.rearrange("(g p t) -> p g t", p=P, t=4))
@@ -208,57 +221,67 @@ def tile_causalwaveletfieldattentionh_pb_l_kernel(tc, q_flat, gathered, Wgate, b
                     acc = acc_pool.tile([P, 512], F32, name="acc", tag="acc")
                     nc.tensor.matmul(out=acc[:], lhsT=ones[:], rhs=bo_src[:, n, :], start=True, stop=True)
                     nc.vector.tensor_copy(out=bo[:, n, :], in_=acc[:])
-            w_copy(0, k, nc.vector.tensor_copy)
-            qcodes[k] = quantize(qg, "q", QC_BUFS)
-            w_quant(0, k)
-        w_copy(1, 2, nc.scalar.copy)
-        w_copy(1, 3, nc.scalar.copy)
+            w_copy((0, k), nc.vector.tensor_copy)
+            quantize(qg, "q", 0, k)
+            w_quant((0, k))
+        w_copy(w_unit(0, 1), nc.scalar.copy)
 
+        waiting = []
         for s in range(STEPS + LAG):
             issue_loads(s + AHEAD)
+            stage1 = s < STEPS
+            stage2 = s >= LAG
+            product = 1 <= s <= STEPS
+            last = s == STEPS + LAG - 1
 
-            w_copy(prep.get(s, 8), 0, nc.vector.tensor_copy)
-            w_copy(prep.get(s, 8), 1, nc.vector.tensor_copy)
-            for k in (2, 0, 3, 1):
-                w_quant(prep.get(s, 8), k)
-
-            if 1 <= s <= STEPS:
-                hg = multiply(sig, g_banks)
-            if s < STEPS:
-                b, g = divmod(s, 4)
+            if product:
+                hg = grp_tile()
+                old_sig, old_banks = sig, g_banks
+                multiply(hg, old_sig, old_banks, 0)
+            for u, qg in waiting:
+                quantize(qg, "q", u // 4, u % 4)
+            waiting = []
+            if stage1:
+                b, g = ORDER[s]
                 sig = work.tile([P, 4, 512], F32, name="sig", tag="sig", bufs=2)
-                accs = mx_groups(
-                    [wcodes[(g, k)] for k in range(4)], [qcodes[4 * b + k] for k in range(4)]
-                )
-                for t in range(4):
-                    nc.scalar.activation(
-                        out=sig[:, t, :], in_=accs[t][:], func=SIGMOID, bias=bg[:, 4 * g + t : 4 * g + t + 1]
-                    )
-            if s + 4 < STEPS:
-                qg = q_transposes(s + 4)
-                qcodes[s + 4] = quantize(qg, "q", QC_BUFS)
-            if 1 <= s <= STEPS:
-                hcodes[s - 1] = quantize(hg, "h", HC_BUFS)
-            if s < STEPS:
-                g_banks = transposes(("g", s), tg_pool, "tg")
-            if s + 1 >= SORT_FROM:
-                if s + 5 < STEPS:
-                    sort_words(("q", s + 5))
-                if s + 1 < STEPS:
-                    sort_words(("g", s + 1))
-            w_copy(prep.get(s + 1, 8), 2, nc.scalar.copy)
-            w_copy(prep.get(s + 1, 8), 3, nc.scalar.copy)
-
-            if s >= LAG:
-                b2, n = divmod(s - LAG, 4)
-                last = s == STEPS + LAG - 1
+            if stage2:
+                b2, n = ORDER[s - LAG]
                 ost = work.tile([P, 4, 512], F32, name="ost", tag="ost", bufs=OUT_BUFS)
-                accs = mx_groups(
-                    [hcodes[4 * b2 + k] for k in range(4)], [wcodes[(4 + n, k)] for k in range(4)]
-                )
-                for tt in range(4):
-                    nc.vector.tensor_tensor(out=ost[:, tt, :], in0=accs[tt][:], in1=bo[:, n, :], op=ADD)
+            for i in range(4):
+                if stage1:
+                    acc = mx_group(("w", g), ("q", b), i)
+                    nc.scalar.activation(
+                        out=sig[:, i, :], in_=acc[:], func=SIGMOID, bias=bg[:, 4 * g + i : 4 * g + i + 1]
+                    )
+                if stage2:
+                    acc = mx_group(("h", b2), ("w", 4 + n), i)
+                    nc.vector.tensor_tensor(out=ost[:, i, :], in0=acc[:], in1=bo[:, n, :], op=ADD)
                     if last:
-                        nc.sync.dma_start(out=out_units[b2, n][:, tt, :], in_=ost[:, tt, :])
-                if not last:
-                    nc.sync.dma_start(out=out_units[b2, n], in_=ost[:])
+                        nc.sync.dma_start(out=out_view[b2, n][:, i, :], in_=ost[:, i, :])
+                if i == 0:
+                    if product:
+                        multiply(hg, old_sig, old_banks, 1)
+                    if s >= SORT_FROM:
+                        for u in q_units(s):
+                            sort_words(("q", u))
+                if i == 1:
+                    w_copy(w_unit(s, 0), nc.vector.tensor_copy)
+                    if product:
+                        quantize(hg, "h", ORDER[s - 1][0], ORDER[s - 1][1])
+                    if s >= SORT_FROM and stage1:
+                        sort_words(("g", s))
+                if i == 2:
+                    w_quant(w_unit(s, 1))
+                    w_quant(w_unit(s, 0))
+            if stage2 and not last:
+                nc.sync.dma_start(out=out_view[b2, n], in_=ost[:])
+
+            for u in q_units(s):
+                waiting.append((u, q_transposes(u)))
+            if stage1:
+                g_banks = transposes(("g", s), tg_pool, "tg")
+            w_copy(w_unit(s + 1, 1), nc.scalar.copy)
+            if s == 0:
+                for u, qg in waiting:
+                    quantize(qg, "q", u // 4, u % 4)
+                waiting = []

from contextlib import ExitStack

import concourse.mybir as mybir
from concourse.masks import make_identity

FLOPS = 2 * 2 * 8192 * 2048 * 2048

F32 = mybir.dt.float32
BF16 = mybir.dt.bfloat16
U32 = mybir.dt.uint32
U8 = mybir.dt.uint8
FP8X4 = mybir.dt.float8_e4m3fn_x4
SIGMOID = mybir.ActivationFunctionType.Sigmoid
MULT = mybir.AluOpType.mult
ADD = mybir.AluOpType.add

P = 128
ORDER = [(s % 2, s // 2) for s in range(8)] + [(b, g) for b in range(2, 16) for g in range(4)]
STEPS = 64
LAG = 8
AHEAD = 2
SORT_FROM = 8
RAW_BUFS = 8
SRT_BUFS = 4
GRP_BUFS = 5
QC_BUFS = 11
QS_BUFS = 4
HC_BUFS = 14
HS_BUFS = 5
OUT_BUFS = 2


def q_units(step):
    if step <= 0:
        return [4 * (step + 1) + k for k in range(4)]
    if 3 <= step < STEPS - 5:
        return [step + 5]
    return []


def w_unit(step, half):
    x = 4 + 2 * step + half
    if step < 0 or x >= 32:
        return None
    return divmod(x, 4)


def tile_causalwaveletfieldattentionh_pb_l_kernel(tc, q_flat, gathered, Wgate, bgate, Wout, bout, out):
    nc = tc.nc
    unit = "(b t p) (g c) -> b g p t c"
    q_view = q_flat.flatten_outer_dims().rearrange(unit, t=4, p=P, c=512)
    g_view = gathered.flatten_outer_dims().rearrange(unit, t=4, p=P, c=512)
    out_view = out.flatten_outer_dims().rearrange(unit, t=4, p=P, c=512)
    w_view = [
        Wgate.rearrange("(k p j) (g c) -> g k p j c", p=P, j=4, c=512),
        Wout.rearrange("(k p j) (g c) -> g k p j c", p=P, j=4, c=512),
    ]

    with ExitStack() as ctx:
        const = ctx.enter_context(tc.tile_pool(name="const", bufs=1))
        work = ctx.enter_context(tc.tile_pool(name="work", bufs=2))
        acc_pool = ctx.enter_context(tc.psum_pool(name="accp", bufs=4))
        tq_pool = ctx.enter_context(tc.psum_pool(name="tqp", bufs=2))
        tg_pool = ctx.enter_context(tc.psum_pool(name="tgp", bufs=2))
        ctx.enter_context(tc.manual_schedule())

        raws = {}
        srts = {}
        grps = {}
        codes = {}
        planes = {}

        def raw_tile():
            return work.tile([P, 4, 512], BF16, name="raw", tag="raw", bufs=RAW_BUFS, align_bytes=64)

        def grp_tile():
            return work.tile([P, 512, 4], BF16, name="grp", tag="grp", bufs=GRP_BUFS, align_bytes=64)

        def load(key, src):
            t = raw_tile()
            nc.sync.dma_start(out=t[:], in_=src)
            raws[key] = t

        def load_w(wk):
            if wk is not None:
                load(("w", wk), w_view[wk[0] // 4][wk[0] % 4, wk[1]])

        def load_step(step):
            for u in q_units(step):
                load(("q", u), q_view[u // 4, u % 4])
            if step < STEPS:
                load(("g", step), g_view[ORDER[step][0], ORDER[step][1]])

        def issue_loads(step):
            if step == -1:
                for k in range(4):
                    load(("q", k), q_view[0, k])
                    load_w((0, k))
            else:
                load_w(w_unit(step, 0))
                load_step(step)
            load_w(w_unit(step + 1, 1))

        def sort_words(key):
            words = raws[key][:].rearrange("p t c -> p (t c)").bitcast(F32)
            srt = work.tile([P, 4, 2, P], F32, name="srt", tag="srt", bufs=SRT_BUFS)
            nc.scalar.copy(out=srt[:], in_=words.rearrange("p (t m u) -> p t u m", t=4, u=2))
            srts[key] = srt

        def transposes(key, pool, tag):
            words = raws[key][:].rearrange("p t c -> p (t c)").bitcast(F32)
            banks = []
            for j in range(2):
                xt = pool.tile([P, 2, 256], F32, name=tag, tag=tag)
                for u in range(2):
                    for i in range(2):
                        tt = 2 * j + i
                        if key in srts:
                            src = srts[key][:, tt, u, :]
                        else:
                            src = words[:, tt * 256 + u : (tt + 1) * 256 : 2]
                        nc.tensor.transpose(xt[:, u, i * P : (i + 1) * P], src, ident[:])
                banks.append(xt)
            return banks

        def quantize(grp, kind, group, k):
            if kind == "w":
                pool, tag, cbufs, sbufs = const, "w%d" % group, 1, 1
                ctag = "w%d%d" % (group, k)
            else:
                pool, tag, ctag = work, kind + "s", kind + "c"
                cbufs, sbufs = (QC_BUFS, QS_BUFS) if kind == "q" else (HC_BUFS, HS_BUFS)
            if (kind, group) not in planes:
                planes[(kind, group)] = pool.tile([P, 512], U8, name=tag, tag=tag, bufs=sbufs, align_bytes=64)
            c = pool.tile([P, 512], U32, name=ctag, tag=ctag, bufs=cbufs, align_bytes=64)
            nc.vector.quantize_mx(
                out=c[:].bitcast(FP8X4),
                scales=planes[(kind, group)][4 * k : P, :],
                in_=grp[:].rearrange("p r j -> p (r j)"),
            )
            codes[(kind, group, k)] = c

        def w_copy(wk, copy):
            if wk is None:
                return
            raw = raws[("w", wk)]
            grp = grp_tile()
            if wk[0] < 4:
                copy(
                    out=grp[:].rearrange("p (t m) j -> p t m j", t=4),
                    in_=raw[:].rearrange("p j (m t) -> p t m j", t=4),
                )
            else:
                copy(out=grp[:], in_=raw[:].rearrange("p j c -> p c j"))
            grps[wk] = grp

        def w_quant(wk):
            if wk is not None:
                quantize(grps[wk], "w", wk[0], wk[1])

        def q_transposes(u):
            banks = transposes(("q", u), tq_pool, "tq")
            grp = grp_tile()
            words = grp[:].rearrange("p r j -> p (r j)").bitcast(F32).rearrange("p (r u) -> p r u", u=2)
            for j in range(2):
                nc.scalar.copy(out=words[:, j * 256 : (j + 1) * 256, :], in_=banks[j][:].rearrange("p u r -> p r u"))
            return grp

        def mx_group(lhs, rhs, i):
            acc = acc_pool.tile([P, 512], F32, name="acc", tag="acc")
            for k in range(4):
                nc.tensor.matmul_mx(
                    out=acc[:],
                    lhsT=codes[lhs + (k,)][:, i * P : (i + 1) * P].bitcast(FP8X4),
                    lhsT_scale=planes[lhs][4 * k : P, i * P : (i + 1) * P],
                    rhs=codes[rhs + (k,)][:].bitcast(FP8X4),
                    rhs_scale=planes[rhs][4 * k : P, :],
                    start=(k == 0),
                    stop=(k == 3),
                )
            return acc

        def multiply(hg, sig, g_banks, j):
            rows = slice(j * 256, (j + 1) * 256)
            nc.vector.tensor_tensor(
                out=hg[:, rows, :].rearrange("p r (u e) -> p r u e", e=2),
                in0=sig[:, :, rows].rearrange("p (u e) r -> p r u e", e=2),
                in1=g_banks[j][:]
                .rearrange("p u r -> p (u r)")
                .bitcast(BF16)
                .rearrange("p (u r e) -> p r u e", u=2, e=2),
                op=MULT,
            )

        bg_bf = const.tile([P, 4, 4], BF16, name="bg_bf", tag="bg_bf")
        nc.scalar.dma_start(out=bg_bf[:], in_=bgate.rearrange("(g p t) -> p g t", p=P, t=4))
        bo_src = raw_tile()
        nc.gpsimd.memset(bo_src[:], 0.0)
        nc.scalar.dma_start(
            out=bo_src[0:1].rearrange("p t c -> p (t c)"), in_=bout.rearrange("(o c) -> o c", o=1)
        )
        warm_in = const.tile([P, 1], F32, name="warm_in", tag="warm_in")
        warm_out = const.tile([P, 1], F32, name="warm_out", tag="warm_out")
        nc.vector.memset(warm_in[:], 0.0)
        nc.scalar.activation(out=warm_out[:], in_=warm_in[:], func=SIGMOID)
        ident = const.tile([P, P], F32, name="ident", tag="ident")
        make_identity(nc, ident[:])
        ones = const.tile([P, P], BF16, name="ones", tag="ones")
        nc.gpsimd.memset(ones[:], 1.0)
        bg = const.tile([P, 16], F32, name="bg", tag="bg")
        nc.vector.tensor_copy(out=bg[:], in_=bg_bf[:].rearrange("p g t -> p (g t)"))
        bo = const.tile([P, 4, 512], F32, name="bo", tag="bo")

        for step in range(-1, AHEAD):
            issue_loads(step)

        for k in range(4):
            qg = q_transposes(k)
            if k == 0:
                for n in range(4):
                    acc = acc_pool.tile([P, 512], F32, name="acc", tag="acc")
                    nc.tensor.matmul(out=acc[:], lhsT=ones[:], rhs=bo_src[:, n, :], start=True, stop=True)
                    nc.vector.tensor_copy(out=bo[:, n, :], in_=acc[:])
            w_copy((0, k), nc.vector.tensor_copy)
            quantize(qg, "q", 0, k)
            w_quant((0, k))
        w_copy(w_unit(0, 1), nc.scalar.copy)

        waiting = []
        for s in range(STEPS + LAG):
            issue_loads(s + AHEAD)
            stage1 = s < STEPS
            stage2 = s >= LAG
            product = 1 <= s <= STEPS
            last = s == STEPS + LAG - 1

            if product:
                hg = grp_tile()
                old_sig, old_banks = sig, g_banks
                multiply(hg, old_sig, old_banks, 0)
            for u, qg in waiting:
                quantize(qg, "q", u // 4, u % 4)
            waiting = []
            if stage1:
                b, g = ORDER[s]
                sig = work.tile([P, 4, 512], F32, name="sig", tag="sig", bufs=2)
            if stage2:
                b2, n = ORDER[s - LAG]
                ost = work.tile([P, 4, 512], F32, name="ost", tag="ost", bufs=OUT_BUFS)
            for i in range(4):
                if stage1:
                    acc = mx_group(("w", g), ("q", b), i)
                    nc.scalar.activation(
                        out=sig[:, i, :], in_=acc[:], func=SIGMOID, bias=bg[:, 4 * g + i : 4 * g + i + 1]
                    )
                if stage2:
                    acc = mx_group(("h", b2), ("w", 4 + n), i)
                    nc.vector.tensor_tensor(out=ost[:, i, :], in0=acc[:], in1=bo[:, n, :], op=ADD)
                    if last:
                        nc.sync.dma_start(out=out_view[b2, n][:, i, :], in_=ost[:, i, :])
                if i == 0:
                    if product:
                        multiply(hg, old_sig, old_banks, 1)
                    if s >= SORT_FROM:
                        for u in q_units(s):
                            sort_words(("q", u))
                if i == 1:
                    w_copy(w_unit(s, 0), nc.vector.tensor_copy)
                    if product:
                        quantize(hg, "h", ORDER[s - 1][0], ORDER[s - 1][1])
                    if s >= SORT_FROM and stage1:
                        sort_words(("g", s))
                if i == 2:
                    w_quant(w_unit(s, 1))
                    w_quant(w_unit(s, 0))
            if stage2 and not last:
                nc.sync.dma_start(out=out_view[b2, n], in_=ost[:])

            for u in q_units(s):
                waiting.append((u, q_transposes(u)))
            if stage1:
                g_banks = transposes(("g", s), tg_pool, "tg")
            w_copy(w_unit(s + 1, 1), nc.scalar.copy)
            if s == 0:
                for u, qg in waiting:
                    quantize(qg, "q", u // 4, u % 4)
                waiting = []
